import numpy as np
import ml_dtypes


def mxq(x, axis, fmt="e4m3"):
    dtype, down = {"e4m3": (ml_dtypes.float8_e4m3fn, 7), "e5m2": (ml_dtypes.float8_e5m2, 14)}[fmt]
    v = np.moveaxis(np.asarray(x, np.float32).astype(ml_dtypes.bfloat16).astype(np.float64), axis, -1)
    blocks = v.reshape(v.shape[:-1] + (-1, 32))
    amax = np.abs(blocks).max(-1, keepdims=True)
    byte = np.maximum(np.where(amax > 0, np.frexp(amax)[1] - 1 + 127, 0) - down, 1)
    scale = np.exp2(byte - 127.0)
    codes = (blocks / scale).astype(np.float32).astype(dtype).astype(np.float64)
    return np.moveaxis((codes * scale).reshape(v.shape), -1, axis)


WIDE = False


def mx_kscale(k):
    if not WIDE:
        return np.ones(k)
    levels = np.array([10, -10, 5, -5, 0])
    a = np.random.permutation(np.resize(levels, k // 512 * 4)).reshape(k // 512, 4)
    idx = np.arange(k)
    return np.exp2(a[idx // 512, idx % 128 // 32])


BF16 = ml_dtypes.bfloat16


def bf(x):
    return np.asarray(x, np.float32).astype(BF16)


def f64(x):
    return np.asarray(x).astype(np.float64)


E2M1 = np.array([0.0, 0.5, 1.0, 1.5, 2.0, 3.0, 4.0, 6.0, -0.0, -0.5, -1.0, -1.5, -2.0, -3.0, -4.0, -6.0])


def pack_weight(w, fmt):
    k, n = w.shape
    w = f64(bf(w)).reshape(k // 32, 32, n)
    amax = np.abs(w).max(1)
    if fmt == "e4m3":
        byte = np.frexp(amax)[1] - 1 + 127 - 7
    else:
        mant, ex = np.frexp(amax / 6.0)
        byte = np.where(mant > 0.5, ex, ex - 1) + 127
    byte = np.clip(np.where(amax > 0, byte, 1), 1, 254)
    scaled = (w * np.exp2(127.0 - byte)[:, None, :]).reshape(k, n).astype(np.float32)
    by_word = np.ascontiguousarray(scaled.reshape(k // 512, 128, 4, n).transpose(0, 1, 3, 2))
    if fmt == "e4m3":
        words = by_word.astype(ml_dtypes.float8_e4m3fn).view(np.uint8)
    else:
        c = by_word.astype(ml_dtypes.float4_e2m1fn).view(np.uint8) & 0xF
        words = c[..., 0::2] | (c[..., 1::2] << 4)
    return np.ascontiguousarray(words), np.ascontiguousarray(byte.astype(np.uint8).reshape(k // 512, 16, n))


def unpack_weight(words, scales, fmt):
    g, p, n, _ = words.shape
    if fmt == "e4m3":
        vals = np.ascontiguousarray(words).view(ml_dtypes.float8_e4m3fn).astype(np.float64)
    else:
        nib = np.empty((g, p, n, 4), np.uint8)
        nib[..., 0::2] = words & 0xF
        nib[..., 1::2] = words >> 4
        vals = E2M1[nib]
    vals = vals * np.repeat(np.exp2(scales.astype(np.float64) - 127.0), 8, axis=1)[..., None]
    return vals.transpose(0, 1, 3, 2).reshape(g * 512, n)


E, I, O, N = 2, 256, 1024, 4096


def setup_inputs():
    s = mx_kscale(O)
    inputs = bf(np.random.standard_normal((E, O, N)) * s[None, :, None])
    stack = np.random.uniform(0.0, 1.0, (E, I, O)) * 1.7 / np.sqrt(O) / s[None, None, :]
    cat = np.ascontiguousarray(stack.swapaxes(1, 2)).reshape(-1, I)
    words, scales = pack_weight(cat, "e4m3")
    return {"inputs": inputs,
            "weight_words": words,
            "weight_scales": scales,
            "expert_size": E}


def reference(inputs, weight_words, weight_scales, expert_size):
    num_experts = E
    chunks = f64(inputs)[:num_experts]
    wq = unpack_weight(weight_words, weight_scales, "e4m3").reshape(E, O, I).swapaxes(1, 2)
    xq = mxq(chunks, 1, "e4m3")
    out = wq[None, :, :, :] @ xq[:, None, :, :]
    C = out.shape[0]
    return out.reshape(C * num_experts, I, inputs.shape[2])

@@ -1,0 +1,137 @@
+from contextlib import ExitStack
+
+import concourse.mybir as mybir
+
+BF16 = mybir.dt.bfloat16
+F32 = mybir.dt.float32
+I32 = mybir.dt.int32
+U32 = mybir.dt.uint32
+U8 = mybir.dt.uint8
+FP8X4 = mybir.dt.float8_e4m3fn_x4
+
+P = 128
+PACK = 4
+K_PASS = P * PACK
+
+CHUNKS = 2
+EXPERTS = 2
+K = 1024
+ROWS = 256
+COLS = 4096
+PASSES = K // K_PASS
+M_TILES = ROWS // P
+PRODUCTS = EXPERTS * M_TILES
+
+N_TILE = 512
+LOAD_COLS = 2048
+UNIT_COLS = 1024
+UNITS_PER_LOAD = LOAD_COLS // UNIT_COLS
+LOADS_AHEAD = 3
+
+RUN = 4
+SCALAR_COLS = UNIT_COLS // 8
+VECTOR_COLS = UNIT_COLS - SCALAR_COLS
+
+FLOPS = 2 * CHUNKS * EXPERTS * ROWS * K * COLS
+
+
+def tile_flaxparallelexperts_t_e_kernel(
+    tc, inputs, weight_words, weight_scales, expert_size, out
+):
+    nc = tc.nc
+    with ExitStack() as pools:
+        keep = pools.enter_context(tc.tile_pool(name="keep", bufs=1))
+        raw_pool = pools.enter_context(tc.tile_pool(name="raw", bufs=LOADS_AHEAD * PASSES))
+        grouped_pool = pools.enter_context(tc.tile_pool(name="grouped", bufs=4))
+        quantised_pool = pools.enter_context(tc.tile_pool(name="quantised", bufs=3))
+        stage_pool = pools.enter_context(tc.tile_pool(name="stage", bufs=3))
+        psum = pools.enter_context(tc.psum_pool(name="psum", bufs=8))
+
+        def load_inputs(c, first_col):
+            tiles = []
+            for g in range(PASSES):
+                raw = raw_pool.tile([P, PACK, LOAD_COLS], BF16)
+                rows = inputs[c, g * K_PASS : (g + 1) * K_PASS, first_col : first_col + LOAD_COLS]
+                nc.sync.dma_start(out=raw[:], in_=rows.rearrange("(p j) w -> p j w", j=PACK))
+                tiles.append(raw)
+            return tiles
+
+        def load_weights():
+            nc.sync.dma_start(
+                out=w_codes[:].bitcast(I32),
+                in_=weight_words.rearrange("g p n t -> p g (n t)").bitcast(I32),
+            )
+            for quadrant in range(4):
+                nc.sync.dma_start(
+                    out=w_scales[32 * quadrant : 32 * quadrant + 4].bitcast(I32),
+                    in_=weight_scales[:, 4 * quadrant : 4 * quadrant + 4, :]
+                    .rearrange("g r n -> r g n")
+                    .bitcast(I32),
+                )
+
+        def regroup(raw, first_col):
+            grouped = grouped_pool.tile([P, UNIT_COLS, PACK], BF16, align_bytes=64)
+            source = raw[:, :, first_col : first_col + UNIT_COLS].rearrange(
+                "p j (w i) -> p w j i", i=RUN
+            )
+            target = grouped[:].rearrange("p (w i) j -> p w j i", i=RUN)
+            split = VECTOR_COLS // RUN
+            nc.vector.tensor_copy(out=target[:, :split], in_=source[:, :split])
+            nc.scalar.copy(out=target[:, split:], in_=source[:, split:])
+            return grouped
+
+        def quantise(grouped, x_codes, x_scales, g):
+            nc.vector.quantize_mx(
+                out=x_codes[:, g, :].bitcast(FP8X4),
+                scales=x_scales[:, g, :],
+                in_=grouped[:].rearrange("p w j -> p (w j)"),
+            )
+
+        def multiply_and_store(x_codes, x_scales, c, first_col):
+            stage = stage_pool.tile([P, PRODUCTS, UNIT_COLS], F32)
+            for n in range(0, UNIT_COLS, N_TILE):
+                for e in range(EXPERTS):
+                    for m in range(M_TILES):
+                        acc = psum.tile([P, N_TILE], F32)
+                        for g in range(PASSES):
+                            nc.tensor.matmul_mx(
+                                out=acc[:],
+                                lhsT=w_codes[:, e * PASSES + g, m * P : (m + 1) * P].bitcast(FP8X4),
+                                lhsT_scale=w_scales[:, e * PASSES + g, m * P : (m + 1) * P],
+                                rhs=x_codes[:, g, n : n + N_TILE].bitcast(FP8X4),
+                                rhs_scale=x_scales[:, g, n : n + N_TILE],
+                                start=(g == 0),
+                                stop=(g == PASSES - 1),
+                            )
+                        nc.scalar.copy(out=stage[:, e * M_TILES + m, n : n + N_TILE], in_=acc[:])
+            rows = out[c * EXPERTS : (c + 1) * EXPERTS].rearrange("e (m p) w -> p (e m) w", p=P)
+            nc.scalar.dma_start(out=rows[:, :, first_col : first_col + UNIT_COLS], in_=stage[:])
+
+        def finish(grouped, x_codes, x_scales, g, c, first_col):
+            quantise(grouped, x_codes, x_scales, g)
+            if g == PASSES - 1:
+                multiply_and_store(x_codes, x_scales, c, first_col)
+
+        w_codes = keep.tile([P, EXPERTS * PASSES, ROWS], U32, align_bytes=64)
+        w_scales = keep.tile([P, EXPERTS * PASSES, ROWS], U8, align_bytes=64)
+        nc.vector.memset(w_scales[:].bitcast(I32), 0)
+
+        ranges = [(c, col) for c in range(CHUNKS) for col in range(0, COLS, LOAD_COLS)]
+        loaded = [load_inputs(*ranges[0])]
+        load_weights()
+        for r in range(1, LOADS_AHEAD):
+            loaded.append(load_inputs(*ranges[r]))
+
+        waiting = None
+        for r, (c, load_col) in enumerate(ranges):
+            for unit_col in range(0, LOAD_COLS, UNIT_COLS):
+                x_codes = quantised_pool.tile([P, PASSES, UNIT_COLS], U32, align_bytes=64)
+                x_scales = quantised_pool.tile([P, PASSES, UNIT_COLS], U8, align_bytes=64)
+                for g in range(PASSES):
+                    grouped = regroup(loaded[r][g], unit_col)
+                    if waiting is not None:
+                        finish(*waiting)
+                    waiting = (grouped, x_codes, x_scales, g, c, load_col + unit_col)
+            if r + LOADS_AHEAD < len(ranges):
+                loaded.append(load_inputs(*ranges[r + LOADS_AHEAD]))
+        finish(*waiting)

@@ -29,8 +29,6 @@ UNITS_PER_LOAD = LOAD_COLS // UNIT_COLS
 LOADS_AHEAD = 3
 
 RUN = 4
-SCALAR_COLS = UNIT_COLS // 8
-VECTOR_COLS = UNIT_COLS - SCALAR_COLS
 
 FLOPS = 2 * CHUNKS * EXPERTS * ROWS * K * COLS
 
@@ -46,6 +44,7 @@ def tile_flaxparallelexperts_t_e_kernel(
         quantised_pool = pools.enter_context(tc.tile_pool(name="quantised", bufs=3))
         stage_pool = pools.enter_context(tc.tile_pool(name="stage", bufs=3))
         psum = pools.enter_context(tc.psum_pool(name="psum", bufs=8))
+        pools.enter_context(tc.manual_schedule())
 
         def load_inputs(c, first_col):
             tiles = []
@@ -75,9 +74,7 @@ def tile_flaxparallelexperts_t_e_kernel(
                 "p j (w i) -> p w j i", i=RUN
             )
             target = grouped[:].rearrange("p (w i) j -> p w j i", i=RUN)
-            split = VECTOR_COLS // RUN
-            nc.vector.tensor_copy(out=target[:, :split], in_=source[:, :split])
-            nc.scalar.copy(out=target[:, split:], in_=source[:, split:])
+            nc.vector.tensor_copy(out=target, in_=source)
             return grouped
 
         def quantise(grouped, x_codes, x_scales, g):
@@ -105,7 +102,7 @@ def tile_flaxparallelexperts_t_e_kernel(
                             )
                         nc.scalar.copy(out=stage[:, e * M_TILES + m, n : n + N_TILE], in_=acc[:])
             rows = out[c * EXPERTS : (c + 1) * EXPERTS].rearrange("e (m p) w -> p (e m) w", p=P)
-            nc.scalar.dma_start(out=rows[:, :, first_col : first_col + UNIT_COLS], in_=stage[:])
+            nc.sync.dma_start(out=rows[:, :, first_col : first_col + UNIT_COLS], in_=stage[:])
 
         def finish(grouped, x_codes, x_scales, g, c, first_col):
             quantise(grouped, x_codes, x_scales, g)

@@ -20,13 +20,11 @@ ROWS = 256
 COLS = 4096
 PASSES = K // K_PASS
 M_TILES = ROWS // P
-PRODUCTS = EXPERTS * M_TILES
 
 N_TILE = 512
-LOAD_COLS = 2048
 UNIT_COLS = 1024
-UNITS_PER_LOAD = LOAD_COLS // UNIT_COLS
-LOADS_AHEAD = 3
+BLOCK_COLS = 2048
+LOAD_COLS = (COLS // 2, COLS)
 
 RUN = 4
 
@@ -38,22 +36,26 @@ def tile_flaxparallelexperts_t_e_kernel(
 ):
     nc = tc.nc
     with ExitStack() as pools:
-        keep = pools.enter_context(tc.tile_pool(name="keep", bufs=1))
-        raw_pool = pools.enter_context(tc.tile_pool(name="raw", bufs=LOADS_AHEAD * PASSES))
-        grouped_pool = pools.enter_context(tc.tile_pool(name="grouped", bufs=4))
-        quantised_pool = pools.enter_context(tc.tile_pool(name="quantised", bufs=3))
-        stage_pool = pools.enter_context(tc.tile_pool(name="stage", bufs=3))
+        resident = pools.enter_context(tc.tile_pool(name="resident", bufs=1))
+        grouped_pool = pools.enter_context(tc.tile_pool(name="grouped", bufs=3))
+        quantised_pool = pools.enter_context(tc.tile_pool(name="quantised", bufs=2))
+        stage_pool = pools.enter_context(tc.tile_pool(name="stage", bufs=4))
         psum = pools.enter_context(tc.psum_pool(name="psum", bufs=8))
         pools.enter_context(tc.manual_schedule())
 
-        def load_inputs(c, first_col):
-            tiles = []
+        w_codes = resident.tile([P, EXPERTS * PASSES, ROWS], U32, align_bytes=64)
+        w_scales = resident.tile([P, EXPERTS * PASSES, ROWS], U8, align_bytes=64)
+        raw_unit = {}
+
+        def load_inputs(c, first_col, width):
             for g in range(PASSES):
-                raw = raw_pool.tile([P, PACK, LOAD_COLS], BF16)
-                rows = inputs[c, g * K_PASS : (g + 1) * K_PASS, first_col : first_col + LOAD_COLS]
+                raw = resident.tile(
+                    [P, PACK, width], BF16, name="raw_c%d_g%d_col%d" % (c, g, first_col)
+                )
+                rows = inputs[c, g * K_PASS : (g + 1) * K_PASS, first_col : first_col + width]
                 nc.sync.dma_start(out=raw[:], in_=rows.rearrange("(p j) w -> p j w", j=PACK))
-                tiles.append(raw)
-            return tiles
+                for col in range(0, width, UNIT_COLS):
+                    raw_unit[c, g, first_col + col] = raw[:, :, col : col + UNIT_COLS]
 
         def load_weights():
             nc.sync.dma_start(
@@ -68,27 +70,19 @@ def tile_flaxparallelexperts_t_e_kernel(
                     .bitcast(I32),
                 )
 
-        def regroup(raw, first_col):
+        def regroup(raw):
             grouped = grouped_pool.tile([P, UNIT_COLS, PACK], BF16, align_bytes=64)
-            source = raw[:, :, first_col : first_col + UNIT_COLS].rearrange(
-                "p j (w i) -> p w j i", i=RUN
+            nc.vector.tensor_copy(
+                out=grouped[:].rearrange("p (w i) j -> p w j i", i=RUN),
+                in_=raw.rearrange("p j (w i) -> p w j i", i=RUN),
             )
-            target = grouped[:].rearrange("p (w i) j -> p w j i", i=RUN)
-            nc.vector.tensor_copy(out=target, in_=source)
             return grouped
 
-        def quantise(grouped, x_codes, x_scales, g):
-            nc.vector.quantize_mx(
-                out=x_codes[:, g, :].bitcast(FP8X4),
-                scales=x_scales[:, g, :],
-                in_=grouped[:].rearrange("p w j -> p (w j)"),
-            )
-
-        def multiply_and_store(x_codes, x_scales, c, first_col):
-            stage = stage_pool.tile([P, PRODUCTS, UNIT_COLS], F32)
-            for n in range(0, UNIT_COLS, N_TILE):
-                for e in range(EXPERTS):
-                    for m in range(M_TILES):
+        def multiply_and_store(x_codes, x_scales, c, block_col):
+            for e in range(EXPERTS):
+                for m in range(M_TILES):
+                    stage = stage_pool.tile([P, BLOCK_COLS], F32)
+                    for n in range(0, BLOCK_COLS, N_TILE):
                         acc = psum.tile([P, N_TILE], F32)
                         for g in range(PASSES):
                             nc.tensor.matmul_mx(
@@ -100,35 +94,44 @@ def tile_flaxparallelexperts_t_e_kernel(
                                 start=(g == 0),
                                 stop=(g == PASSES - 1),
                             )
-                        nc.scalar.copy(out=stage[:, e * M_TILES + m, n : n + N_TILE], in_=acc[:])
-            rows = out[c * EXPERTS : (c + 1) * EXPERTS].rearrange("e (m p) w -> p (e m) w", p=P)
-            nc.sync.dma_start(out=rows[:, :, first_col : first_col + UNIT_COLS], in_=stage[:])
+                        nc.scalar.copy(out=stage[:, n : n + N_TILE], in_=acc[:])
+                    nc.sync.dma_start(
+                        out=out[
+                            c * EXPERTS + e, m * P : (m + 1) * P, block_col : block_col + BLOCK_COLS
+                        ],
+                        in_=stage[:],
+                    )
 
-        def finish(grouped, x_codes, x_scales, g, c, first_col):
-            quantise(grouped, x_codes, x_scales, g)
-            if g == PASSES - 1:
-                multiply_and_store(x_codes, x_scales, c, first_col)
+        def finish(grouped, x_codes, x_scales, g, col, c, block_col):
+            nc.vector.quantize_mx(
+                out=x_codes[:, g, col : col + UNIT_COLS].bitcast(FP8X4),
+                scales=x_scales[:, g, col : col + UNIT_COLS],
+                in_=grouped[:].rearrange("p w j -> p (w j)"),
+            )
+            if g == PASSES - 1 and col + UNIT_COLS == BLOCK_COLS:
+                multiply_and_store(x_codes, x_scales, c, block_col)
 
-        w_codes = keep.tile([P, EXPERTS * PASSES, ROWS], U32, align_bytes=64)
-        w_scales = keep.tile([P, EXPERTS * PASSES, ROWS], U8, align_bytes=64)
         nc.vector.memset(w_scales[:].bitcast(I32), 0)
 
-        ranges = [(c, col) for c in range(CHUNKS) for col in range(0, COLS, LOAD_COLS)]
-        loaded = [load_inputs(*ranges[0])]
+        loads = [
+            (c, first_col, LOAD_COLS[c])
+            for c in range(CHUNKS)
+            for first_col in range(0, COLS, LOAD_COLS[c])
+        ]
+        load_inputs(*loads[0])
         load_weights()
-        for r in range(1, LOADS_AHEAD):
-            loaded.append(load_inputs(*ranges[r]))
+        for load in loads[1:]:
+            load_inputs(*load)
 
         waiting = None
-        for r, (c, load_col) in enumerate(ranges):
-            for unit_col in range(0, LOAD_COLS, UNIT_COLS):
-                x_codes = quantised_pool.tile([P, PASSES, UNIT_COLS], U32, align_bytes=64)
-                x_scales = quantised_pool.tile([P, PASSES, UNIT_COLS], U8, align_bytes=64)
+        for c in range(CHUNKS):
+            for block_col in range(0, COLS, BLOCK_COLS):
+                x_codes = quantised_pool.tile([P, PASSES, BLOCK_COLS], U32, align_bytes=64)
+                x_scales = quantised_pool.tile([P, PASSES, BLOCK_COLS], U8, align_bytes=64)
                 for g in range(PASSES):
-                    grouped = regroup(loaded[r][g], unit_col)
-                    if waiting is not None:
-                        finish(*waiting)
-                    waiting = (grouped, x_codes, x_scales, g, c, load_col + unit_col)
-            if r + LOADS_AHEAD < len(ranges):
-                loaded.append(load_inputs(*ranges[r + LOADS_AHEAD]))
+                    for col in range(0, BLOCK_COLS, UNIT_COLS):
+                        grouped = regroup(raw_unit[c, g, block_col + col])
+                        if waiting is not None:
+                            finish(*waiting)
+                        waiting = (grouped, x_codes, x_scales, g, col, c, block_col)
         finish(*waiting)

@@ -26,6 +26,14 @@ UNIT_COLS = 1024
 BLOCK_COLS = 2048
 LOAD_COLS = (COLS // 2, COLS)
 
+BLOCKS = (
+    (0, 0, BLOCK_COLS),
+    (0, BLOCK_COLS, BLOCK_COLS),
+    (1, 0, BLOCK_COLS),
+    (1, BLOCK_COLS, UNIT_COLS),
+    (1, BLOCK_COLS + UNIT_COLS, UNIT_COLS),
+)
+
 RUN = 4
 
 FLOPS = 2 * CHUNKS * EXPERTS * ROWS * K * COLS
@@ -102,13 +110,54 @@ def tile_flaxparallelexperts_t_e_kernel(
                         in_=stage[:],
                     )
 
-        def finish(grouped, x_codes, x_scales, g, col, c, block_col):
+        def one_pass(acc, x_codes, x_scales, e, m, g, n):
+            nc.tensor.matmul_mx(
+                out=acc[:],
+                lhsT=w_codes[:, e * PASSES + g, m * P : (m + 1) * P].bitcast(FP8X4),
+                lhsT_scale=w_scales[:, e * PASSES + g, m * P : (m + 1) * P],
+                rhs=x_codes[:, g, n : n + N_TILE].bitcast(FP8X4),
+                rhs_scale=x_scales[:, g, n : n + N_TILE],
+                start=(g == 0),
+                stop=(g == PASSES - 1),
+            )
+
+        open_groups = {}
+
+        def follow(x_codes, x_scales, g, c, block_col, last):
+            for e in range(EXPERTS):
+                for m in range(M_TILES):
+                    if g == PASSES - 1:
+                        stage = stage_pool.tile([P, UNIT_COLS], F32, name="stage")
+                    for n in range(0, UNIT_COLS, N_TILE):
+                        if g == 0:
+                            acc = psum.tile([P, N_TILE], F32, name="acc")
+                            open_groups[e, m, n] = acc
+                        acc = open_groups[e, m, n]
+                        one_pass(acc, x_codes, x_scales, e, m, g, n)
+                        if g == PASSES - 1:
+                            if last and n // N_TILE % 2 == 1:
+                                nc.vector.tensor_copy(out=stage[:, n : n + N_TILE], in_=acc[:])
+                            else:
+                                nc.scalar.copy(out=stage[:, n : n + N_TILE], in_=acc[:])
+                    if g == PASSES - 1:
+                        nc.sync.dma_start(
+                            out=out[
+                                c * EXPERTS + e,
+                                m * P : (m + 1) * P,
+                                block_col : block_col + UNIT_COLS,
+                            ],
+                            in_=stage[:],
+                        )
+
+        def finish(grouped, x_codes, x_scales, g, col, c, block_col, width, last):
             nc.vector.quantize_mx(
                 out=x_codes[:, g, col : col + UNIT_COLS].bitcast(FP8X4),
                 scales=x_scales[:, g, col : col + UNIT_COLS],
                 in_=grouped[:].rearrange("p w j -> p (w j)"),
             )
-            if g == PASSES - 1 and col + UNIT_COLS == BLOCK_COLS:
+            if width == UNIT_COLS:
+                follow(x_codes, x_scales, g, c, block_col, last)
+            elif g == PASSES - 1 and col + UNIT_COLS == width:
                 multiply_and_store(x_codes, x_scales, c, block_col)
 
         nc.vector.memset(w_scales[:].bitcast(I32), 0)
@@ -124,14 +173,14 @@ def tile_flaxparallelexperts_t_e_kernel(
             load_inputs(*load)
 
         waiting = None
-        for c in range(CHUNKS):
-            for block_col in range(0, COLS, BLOCK_COLS):
-                x_codes = quantised_pool.tile([P, PASSES, BLOCK_COLS], U32, align_bytes=64)
-                x_scales = quantised_pool.tile([P, PASSES, BLOCK_COLS], U8, align_bytes=64)
-                for g in range(PASSES):
-                    for col in range(0, BLOCK_COLS, UNIT_COLS):
-                        grouped = regroup(raw_unit[c, g, block_col + col])
-                        if waiting is not None:
-                            finish(*waiting)
-                        waiting = (grouped, x_codes, x_scales, g, col, c, block_col)
+        for c, block_col, width in BLOCKS:
+            x_codes = quantised_pool.tile([P, PASSES, width], U32, align_bytes=64, name="x_codes")
+            x_scales = quantised_pool.tile([P, PASSES, width], U8, align_bytes=64, name="x_scales")
+            last = (c, block_col, width) == BLOCKS[-1]
+            for g in range(PASSES):
+                for col in range(0, width, UNIT_COLS):
+                    grouped = regroup(raw_unit[c, g, block_col + col])
+                    if waiting is not None:
+                        finish(*waiting)
+                    waiting = (grouped, x_codes, x_scales, g, col, c, block_col, width, last)
         finish(*waiting)

@@ -47,7 +47,7 @@ def tile_flaxparallelexperts_t_e_kernel(
         resident = pools.enter_context(tc.tile_pool(name="resident", bufs=1))
         grouped_pool = pools.enter_context(tc.tile_pool(name="grouped", bufs=3))
         quantised_pool = pools.enter_context(tc.tile_pool(name="quantised", bufs=2))
-        stage_pool = pools.enter_context(tc.tile_pool(name="stage", bufs=4))
+        big_pool = pools.enter_context(tc.tile_pool(name="big", bufs=CHUNKS * PASSES + 1))
         psum = pools.enter_context(tc.psum_pool(name="psum", bufs=8))
         pools.enter_context(tc.manual_schedule())
 
@@ -55,13 +55,16 @@ def tile_flaxparallelexperts_t_e_kernel(
         w_scales = resident.tile([P, EXPERTS * PASSES, ROWS], U8, align_bytes=64)
         raw_unit = {}
 
+        raw_tiles = {}
+
         def load_inputs(c, first_col, width):
             for g in range(PASSES):
-                raw = resident.tile(
-                    [P, PACK, width], BF16, name="raw_c%d_g%d_col%d" % (c, g, first_col)
-                )
+                if first_col == 0:
+                    raw_tile = big_pool.tile([P, COLS // width, PACK, width], BF16, name="big")
+                    raw_tiles[c, g] = raw_tile
+                raw = raw_tiles[c, g][:, first_col // width]
                 rows = inputs[c, g * K_PASS : (g + 1) * K_PASS, first_col : first_col + width]
-                nc.sync.dma_start(out=raw[:], in_=rows.rearrange("(p j) w -> p j w", j=PACK))
+                nc.sync.dma_start(out=raw, in_=rows.rearrange("(p j) w -> p j w", j=PACK))
                 for col in range(0, width, UNIT_COLS):
                     raw_unit[c, g, first_col + col] = raw[:, :, col : col + UNIT_COLS]
 
@@ -87,9 +90,10 @@ def tile_flaxparallelexperts_t_e_kernel(
             return grouped
 
         def multiply_and_store(x_codes, x_scales, c, block_col):
+            stages = big_pool.tile([P, EXPERTS * M_TILES, BLOCK_COLS], F32, name="big")
             for e in range(EXPERTS):
                 for m in range(M_TILES):
-                    stage = stage_pool.tile([P, BLOCK_COLS], F32)
+                    stage = stages[:, e * M_TILES + m]
                     for n in range(0, BLOCK_COLS, N_TILE):
                         acc = psum.tile([P, N_TILE], F32)
                         for g in range(PASSES):
@@ -107,7 +111,7 @@ def tile_flaxparallelexperts_t_e_kernel(
                         out=out[
                             c * EXPERTS + e, m * P : (m + 1) * P, block_col : block_col + BLOCK_COLS
                         ],
-                        in_=stage[:],
+                        in_=stage,
                     )
 
         def one_pass(acc, x_codes, x_scales, e, m, g, n):
@@ -124,10 +128,13 @@ def tile_flaxparallelexperts_t_e_kernel(
         open_groups = {}
 
         def follow(x_codes, x_scales, g, c, block_col, last):
+            stages = None
+            if g == PASSES - 1:
+                stages = big_pool.tile([P, EXPERTS * M_TILES, UNIT_COLS], F32, name="big")
             for e in range(EXPERTS):
                 for m in range(M_TILES):
                     if g == PASSES - 1:
-                        stage = stage_pool.tile([P, UNIT_COLS], F32, name="stage")
+                        stage = stages[:, e * M_TILES + m]
                     for n in range(0, UNIT_COLS, N_TILE):
                         if g == 0:
                             acc = psum.tile([P, N_TILE], F32, name="acc")
@@ -146,7 +153,7 @@ def tile_flaxparallelexperts_t_e_kernel(
                                 m * P : (m + 1) * P,
                                 block_col : block_col + UNIT_COLS,
                             ],
-                            in_=stage[:],
+                            in_=stage,
                         )
 
         def finish(grouped, x_codes, x_scales, g, col, c, block_col, width, last):

@@ -24,15 +24,12 @@ M_TILES = ROWS // P
 N_TILE = 512
 UNIT_COLS = 1024
 BLOCK_COLS = 2048
-LOAD_COLS = (COLS // 2, COLS)
+UNITS = COLS // UNIT_COLS
 
-BLOCKS = (
-    (0, 0, BLOCK_COLS),
-    (0, BLOCK_COLS, BLOCK_COLS),
-    (1, 0, BLOCK_COLS),
-    (1, BLOCK_COLS, UNIT_COLS),
-    (1, BLOCK_COLS + UNIT_COLS, UNIT_COLS),
-)
+RAW_BYTES = PACK * COLS * 2
+ARENA_BYTES = PASSES * RAW_BYTES
+
+SCALAR_UNITS = (1, 3, 5)
 
 RUN = 4
 
@@ -45,28 +42,23 @@ def tile_flaxparallelexperts_t_e_kernel(
     nc = tc.nc
     with ExitStack() as pools:
         resident = pools.enter_context(tc.tile_pool(name="resident", bufs=1))
-        grouped_pool = pools.enter_context(tc.tile_pool(name="grouped", bufs=3))
-        quantised_pool = pools.enter_context(tc.tile_pool(name="quantised", bufs=2))
-        big_pool = pools.enter_context(tc.tile_pool(name="big", bufs=CHUNKS * PASSES + 1))
+        arena = pools.enter_context(tc.tile_pool(name="arena", bufs=1))
+        grouped_pool = pools.enter_context(tc.tile_pool(name="grouped", bufs=4))
+        quantised_pool = pools.enter_context(tc.tile_pool(name="quantised", bufs=3))
         psum = pools.enter_context(tc.psum_pool(name="psum", bufs=8))
         pools.enter_context(tc.manual_schedule())
 
         w_codes = resident.tile([P, EXPERTS * PASSES, ROWS], U32, align_bytes=64)
         w_scales = resident.tile([P, EXPERTS * PASSES, ROWS], U8, align_bytes=64)
-        raw_unit = {}
 
-        raw_tiles = {}
-
-        def load_inputs(c, first_col, width):
-            for g in range(PASSES):
-                if first_col == 0:
-                    raw_tile = big_pool.tile([P, COLS // width, PACK, width], BF16, name="big")
-                    raw_tiles[c, g] = raw_tile
-                raw = raw_tiles[c, g][:, first_col // width]
-                rows = inputs[c, g * K_PASS : (g + 1) * K_PASS, first_col : first_col + width]
-                nc.sync.dma_start(out=raw, in_=rows.rearrange("(p j) w -> p j w", j=PACK))
-                for col in range(0, width, UNIT_COLS):
-                    raw_unit[c, g, first_col + col] = raw[:, :, col : col + UNIT_COLS]
+        def load_inputs(c, g):
+            if c == 0:
+                raw = arena.tile([P, PACK, COLS], BF16, name="raw_c0_g%d" % g, offset=g * RAW_BYTES)
+            else:
+                raw = resident.tile([P, PACK, COLS], BF16, name="raw_c1_g%d" % g)
+            rows = inputs[c, g * K_PASS : (g + 1) * K_PASS, :]
+            nc.sync.dma_start(out=raw[:], in_=rows.rearrange("(p j) w -> p j w", j=PACK))
+            return raw
 
         def load_weights():
             nc.sync.dma_start(
@@ -81,40 +73,31 @@ def tile_flaxparallelexperts_t_e_kernel(
                     .bitcast(I32),
                 )
 
-        def regroup(raw):
-            grouped = grouped_pool.tile([P, UNIT_COLS, PACK], BF16, align_bytes=64)
-            nc.vector.tensor_copy(
-                out=grouped[:].rearrange("p (w i) j -> p w j i", i=RUN),
-                in_=raw.rearrange("p j (w i) -> p w j i", i=RUN),
-            )
+        def regroup(raw, col, on_scalar):
+            grouped = grouped_pool.tile([P, UNIT_COLS, PACK], BF16, align_bytes=64, name="grouped")
+            dst = grouped[:].rearrange("p (w i) j -> p w j i", i=RUN)
+            src = raw[:, :, col : col + UNIT_COLS].rearrange("p j (w i) -> p w j i", i=RUN)
+            if on_scalar:
+                nc.scalar.copy(out=dst, in_=src)
+            else:
+                nc.vector.tensor_copy(out=dst, in_=src)
             return grouped
 
-        def multiply_and_store(x_codes, x_scales, c, block_col):
-            stages = big_pool.tile([P, EXPERTS * M_TILES, BLOCK_COLS], F32, name="big")
-            for e in range(EXPERTS):
-                for m in range(M_TILES):
-                    stage = stages[:, e * M_TILES + m]
-                    for n in range(0, BLOCK_COLS, N_TILE):
-                        acc = psum.tile([P, N_TILE], F32)
-                        for g in range(PASSES):
-                            nc.tensor.matmul_mx(
-                                out=acc[:],
-                                lhsT=w_codes[:, e * PASSES + g, m * P : (m + 1) * P].bitcast(FP8X4),
-                                lhsT_scale=w_scales[:, e * PASSES + g, m * P : (m + 1) * P],
-                                rhs=x_codes[:, g, n : n + N_TILE].bitcast(FP8X4),
-                                rhs_scale=x_scales[:, g, n : n + N_TILE],
-                                start=(g == 0),
-                                stop=(g == PASSES - 1),
-                            )
-                        nc.scalar.copy(out=stage[:, n : n + N_TILE], in_=acc[:])
-                    nc.sync.dma_start(
-                        out=out[
-                            c * EXPERTS + e, m * P : (m + 1) * P, block_col : block_col + BLOCK_COLS
-                        ],
-                        in_=stage,
-                    )
+        def new_block():
+            x_codes = quantised_pool.tile([P, PASSES, BLOCK_COLS], U32, align_bytes=64, name="x_codes")
+            x_scales = quantised_pool.tile([P, PASSES, BLOCK_COLS], U8, align_bytes=64, name="x_scales")
+            return x_codes, x_scales
 
-        def one_pass(acc, x_codes, x_scales, e, m, g, n):
+        def quantise(grouped, block, g, col):
+            x_codes, x_scales = block
+            nc.vector.quantize_mx(
+                out=x_codes[:, g, col : col + UNIT_COLS].bitcast(FP8X4),
+                scales=x_scales[:, g, col : col + UNIT_COLS],
+                in_=grouped[:].rearrange("p w j -> p (w j)"),
+            )
+
+        def one_pass(acc, block, e, m, g, n):
+            x_codes, x_scales = block
             nc.tensor.matmul_mx(
                 out=acc[:],
                 lhsT=w_codes[:, e * PASSES + g, m * P : (m + 1) * P].bitcast(FP8X4),
@@ -125,69 +108,92 @@ def tile_flaxparallelexperts_t_e_kernel(
                 stop=(g == PASSES - 1),
             )
 
+        staged_bytes = [0]
+
+        def new_stage(width):
+            first_byte = staged_bytes[0]
+            staged_bytes[0] = first_byte + M_TILES * width * 4
+            return arena.tile(
+                [P, M_TILES, width],
+                F32,
+                name="stage_%d" % first_byte,
+                offset=first_byte % ARENA_BYTES,
+            )
+
+        def store(stage, c, e, m, first_col, width):
+            nc.sync.dma_start(
+                out=out[c * EXPERTS + e, m * P : (m + 1) * P, first_col : first_col + width],
+                in_=stage[:, m],
+            )
+
+        def multiply_and_store(block, c, block_col):
+            for e in range(EXPERTS):
+                stage = new_stage(BLOCK_COLS)
+                for m in range(M_TILES):
+                    for n in range(0, BLOCK_COLS, N_TILE):
+                        acc = psum.tile([P, N_TILE], F32, name="acc")
+                        for g in range(PASSES):
+                            one_pass(acc, block, e, m, g, n)
+                        nc.scalar.copy(out=stage[:, m, n : n + N_TILE], in_=acc[:])
+                    store(stage, c, e, m, block_col, BLOCK_COLS)
+
         open_groups = {}
 
-        def follow(x_codes, x_scales, g, c, block_col, last):
-            stages = None
-            if g == PASSES - 1:
-                stages = big_pool.tile([P, EXPERTS * M_TILES, UNIT_COLS], F32, name="big")
+        def follow(block, g, col, c, block_col):
+            last = col + UNIT_COLS == BLOCK_COLS
             for e in range(EXPERTS):
+                stage = None
+                if g == PASSES - 1:
+                    stage = new_stage(UNIT_COLS)
                 for m in range(M_TILES):
-                    if g == PASSES - 1:
-                        stage = stages[:, e * M_TILES + m]
-                    for n in range(0, UNIT_COLS, N_TILE):
+                    for n in range(col, col + UNIT_COLS, N_TILE):
                         if g == 0:
                             acc = psum.tile([P, N_TILE], F32, name="acc")
                             open_groups[e, m, n] = acc
                         acc = open_groups[e, m, n]
-                        one_pass(acc, x_codes, x_scales, e, m, g, n)
+                        one_pass(acc, block, e, m, g, n)
                         if g == PASSES - 1:
+                            dst = stage[:, m, n - col : n - col + N_TILE]
                             if last and n // N_TILE % 2 == 1:
-                                nc.vector.tensor_copy(out=stage[:, n : n + N_TILE], in_=acc[:])
+                                nc.vector.tensor_copy(out=dst, in_=acc[:])
                             else:
-                                nc.scalar.copy(out=stage[:, n : n + N_TILE], in_=acc[:])
+                                nc.scalar.copy(out=dst, in_=acc[:])
                     if g == PASSES - 1:
-                        nc.sync.dma_start(
-                            out=out[
-                                c * EXPERTS + e,
-                                m * P : (m + 1) * P,
-                                block_col : block_col + UNIT_COLS,
-                            ],
-                            in_=stage,
-                        )
-
-        def finish(grouped, x_codes, x_scales, g, col, c, block_col, width, last):
-            nc.vector.quantize_mx(
-                out=x_codes[:, g, col : col + UNIT_COLS].bitcast(FP8X4),
-                scales=x_scales[:, g, col : col + UNIT_COLS],
-                in_=grouped[:].rearrange("p w j -> p (w j)"),
-            )
-            if width == UNIT_COLS:
-                follow(x_codes, x_scales, g, c, block_col, last)
-            elif g == PASSES - 1 and col + UNIT_COLS == width:
-                multiply_and_store(x_codes, x_scales, c, block_col)
+                        store(stage, c, e, m, block_col + col, UNIT_COLS)
 
         nc.vector.memset(w_scales[:].bitcast(I32), 0)
 
-        loads = [
-            (c, first_col, LOAD_COLS[c])
-            for c in range(CHUNKS)
-            for first_col in range(0, COLS, LOAD_COLS[c])
-        ]
-        load_inputs(*loads[0])
+        raw = {}
+        raw[0, 0] = load_inputs(0, 0)
+        raw[0, 1] = load_inputs(0, 1)
         load_weights()
-        for load in loads[1:]:
-            load_inputs(*load)
+        raw[1, 0] = load_inputs(1, 0)
+        raw[1, 1] = load_inputs(1, 1)
+
+        halves = range(0, COLS, BLOCK_COLS)
+        in_block = range(0, BLOCK_COLS, UNIT_COLS)
+        blocks = {}
+        for c in range(CHUNKS):
+            for block_col in halves:
+                blocks[c, block_col] = None
+        units = [(0, g, col, block_col) for g in range(PASSES) for block_col in halves for col in in_block]
+        units += [(1, g, col, 0) for g in range(PASSES) for col in in_block]
+        units += [(1, g, col, BLOCK_COLS) for col in in_block for g in range(PASSES)]
+
+        def finish(grouped, c, g, col, block_col):
+            block = blocks[c, block_col]
+            quantise(grouped, block, g, col)
+            if (c, block_col) == (CHUNKS - 1, COLS - BLOCK_COLS):
+                follow(block, g, col, c, block_col)
+            elif g == PASSES - 1 and col + UNIT_COLS == BLOCK_COLS:
+                multiply_and_store(block, c, block_col)
 
         waiting = None
-        for c, block_col, width in BLOCKS:
-            x_codes = quantised_pool.tile([P, PASSES, width], U32, align_bytes=64, name="x_codes")
-            x_scales = quantised_pool.tile([P, PASSES, width], U8, align_bytes=64, name="x_scales")
-            last = (c, block_col, width) == BLOCKS[-1]
-            for g in range(PASSES):
-                for col in range(0, width, UNIT_COLS):
-                    grouped = regroup(raw_unit[c, g, block_col + col])
-                    if waiting is not None:
-                        finish(*waiting)
-                    waiting = (grouped, x_codes, x_scales, g, col, c, block_col, width, last)
+        for i, (c, g, col, block_col) in enumerate(units):
+            if blocks[c, block_col] is None:
+                blocks[c, block_col] = new_block()
+            grouped = regroup(raw[c, g], block_col + col, on_scalar=(i in SCALAR_UNITS))
+            if waiting is not None:
+                finish(*waiting)
+            waiting = (grouped, c, g, col, block_col)
         finish(*waiting)

@@ -109,6 +109,7 @@ def tile_flaxparallelexperts_t_e_kernel(
             )
 
         staged_bytes = [0]
+        wide_stages = {}
 
         def new_stage(width):
             first_byte = staged_bytes[0]
@@ -125,6 +126,20 @@ def tile_flaxparallelexperts_t_e_kernel(
                 out=out[c * EXPERTS + e, m * P : (m + 1) * P, first_col : first_col + width],
                 in_=stage[:, m],
             )
+
+        def first_chunk_products(e, cols):
+            if cols[0] == 0:
+                wide_stages[e] = new_stage(COLS)
+            stage = wide_stages[e]
+            for m in range(M_TILES):
+                for n in cols:
+                    block = blocks[0, n // BLOCK_COLS * BLOCK_COLS]
+                    acc = psum.tile([P, N_TILE], F32, name="acc")
+                    for g in range(PASSES):
+                        one_pass(acc, block, e, m, g, n % BLOCK_COLS)
+                    nc.scalar.copy(out=stage[:, m, n : n + N_TILE], in_=acc[:])
+                if cols[-1] + N_TILE == COLS:
+                    store(stage, 0, e, m, 0, COLS)
 
         def multiply_and_store(block, c, block_col):
             for e in range(EXPERTS):
@@ -185,6 +200,11 @@ def tile_flaxparallelexperts_t_e_kernel(
             quantise(grouped, block, g, col)
             if (c, block_col) == (CHUNKS - 1, COLS - BLOCK_COLS):
                 follow(block, g, col, c, block_col)
+            elif c == 0 and g == PASSES - 1:
+                first_col = block_col + col
+                first_chunk_products(0, list(range(first_col, first_col + UNIT_COLS, N_TILE)))
+                if first_col + UNIT_COLS == COLS:
+                    first_chunk_products(1, list(range(0, COLS, N_TILE)))
             elif g == PASSES - 1 and col + UNIT_COLS == BLOCK_COLS:
                 multiply_and_store(block, c, block_col)
 
@@ -192,6 +212,9 @@ def tile_flaxparallelexperts_t_e_kernel(
         for i, (c, g, col, block_col) in enumerate(units):
             if blocks[c, block_col] is None:
                 blocks[c, block_col] = new_block()
+            if waiting is not None and waiting[1] != c:
+                finish(*waiting)
+                waiting = None
             grouped = regroup(raw[c, g], block_col + col, on_scalar=(i in SCALAR_UNITS))
             if waiting is not None:
                 finish(*waiting)

@@ -49,7 +49,7 @@ def tile_flaxparallelexperts_t_e_kernel(
         pools.enter_context(tc.manual_schedule())
 
         w_codes = resident.tile([P, EXPERTS * PASSES, ROWS], U32, align_bytes=64)
-        w_scales = resident.tile([P, EXPERTS * PASSES, ROWS], U8, align_bytes=64)
+        w_scales = resident.tile([P, ROWS], U8, align_bytes=64)
 
         def load_inputs(c, g):
             if c == 0:
@@ -67,10 +67,8 @@ def tile_flaxparallelexperts_t_e_kernel(
             )
             for quadrant in range(4):
                 nc.sync.dma_start(
-                    out=w_scales[32 * quadrant : 32 * quadrant + 4].bitcast(I32),
-                    in_=weight_scales[:, 4 * quadrant : 4 * quadrant + 4, :]
-                    .rearrange("g r n -> r g n")
-                    .bitcast(I32),
+                    out=w_scales[32 * quadrant : 32 * quadrant + 16].bitcast(I32),
+                    in_=weight_scales[:, 4 * quadrant : 4 * quadrant + 4, :].bitcast(I32),
                 )
 
         def regroup(raw, col, on_scalar):
@@ -101,7 +99,7 @@ def tile_flaxparallelexperts_t_e_kernel(
             nc.tensor.matmul_mx(
                 out=acc[:],
                 lhsT=w_codes[:, e * PASSES + g, m * P : (m + 1) * P].bitcast(FP8X4),
-                lhsT_scale=w_scales[:, e * PASSES + g, m * P : (m + 1) * P],
+                lhsT_scale=w_scales[4 * (e * PASSES + g) :, m * P : (m + 1) * P],
                 rhs=x_codes[:, g, n : n + N_TILE].bitcast(FP8X4),
                 rhs_scale=x_scales[:, g, n : n + N_TILE],
                 start=(g == 0),

@@ -107,48 +107,54 @@ def tile_flaxparallelexperts_t_e_kernel(
             )
 
         staged_bytes = [0]
-        wide_stages = {}
 
         def new_stage(width):
-            first_byte = staged_bytes[0]
-            staged_bytes[0] = first_byte + M_TILES * width * 4
-            return arena.tile(
-                [P, M_TILES, width],
-                F32,
-                name="stage_%d" % first_byte,
-                offset=first_byte % ARENA_BYTES,
-            )
+            stage = []
+            for m in range(M_TILES):
+                first_byte = staged_bytes[0]
+                staged_bytes[0] = first_byte + width * 4
+                stage.append(
+                    arena.tile(
+                        [P, width],
+                        F32,
+                        name="stage_%d" % first_byte,
+                        offset=first_byte % ARENA_BYTES,
+                    )
+                )
+            return stage
 
         def store(stage, c, e, m, first_col, width):
             nc.sync.dma_start(
                 out=out[c * EXPERTS + e, m * P : (m + 1) * P, first_col : first_col + width],
-                in_=stage[:, m],
+                in_=stage[m][:],
             )
 
-        def first_chunk_products(e, cols):
-            if cols[0] == 0:
-                wide_stages[e] = new_stage(COLS)
-            stage = wide_stages[e]
+        def multiply_chunk(c, e):
+            stage = new_stage(COLS)
             for m in range(M_TILES):
-                for n in cols:
-                    block = blocks[0, n // BLOCK_COLS * BLOCK_COLS]
+                for n in range(0, COLS, N_TILE):
+                    block = blocks[c, n // BLOCK_COLS * BLOCK_COLS]
                     acc = psum.tile([P, N_TILE], F32, name="acc")
                     for g in range(PASSES):
                         one_pass(acc, block, e, m, g, n % BLOCK_COLS)
-                    nc.scalar.copy(out=stage[:, m, n : n + N_TILE], in_=acc[:])
-                if cols[-1] + N_TILE == COLS:
-                    store(stage, 0, e, m, 0, COLS)
+                    nc.scalar.copy(out=stage[m][:, n : n + N_TILE], in_=acc[:])
+                store(stage, c, e, m, 0, COLS)
 
-        def multiply_and_store(block, c, block_col):
-            for e in range(EXPERTS):
-                stage = new_stage(BLOCK_COLS)
+        block_stages = {}
+
+        def multiply_unit(block, col, c, block_col, experts):
+            for e in experts:
+                if col == 0:
+                    block_stages[e] = new_stage(BLOCK_COLS)
+                stage = block_stages[e]
                 for m in range(M_TILES):
-                    for n in range(0, BLOCK_COLS, N_TILE):
+                    for n in range(col, col + UNIT_COLS, N_TILE):
                         acc = psum.tile([P, N_TILE], F32, name="acc")
                         for g in range(PASSES):
                             one_pass(acc, block, e, m, g, n)
-                        nc.scalar.copy(out=stage[:, m, n : n + N_TILE], in_=acc[:])
-                    store(stage, c, e, m, block_col, BLOCK_COLS)
+                        nc.scalar.copy(out=stage[m][:, n : n + N_TILE], in_=acc[:])
+                    if col + UNIT_COLS == BLOCK_COLS:
+                        store(stage, c, e, m, block_col, BLOCK_COLS)
 
         open_groups = {}
 
@@ -166,7 +172,7 @@ def tile_flaxparallelexperts_t_e_kernel(
                         acc = open_groups[e, m, n]
                         one_pass(acc, block, e, m, g, n)
                         if g == PASSES - 1:
-                            dst = stage[:, m, n - col : n - col + N_TILE]
+                            dst = stage[m][:, n - col : n - col + N_TILE]
                             if last and n // N_TILE % 2 == 1:
                                 nc.vector.tensor_copy(out=dst, in_=acc[:])
                             else:
@@ -199,18 +205,17 @@ def tile_flaxparallelexperts_t_e_kernel(
             if (c, block_col) == (CHUNKS - 1, COLS - BLOCK_COLS):
                 follow(block, g, col, c, block_col)
             elif c == 0 and g == PASSES - 1:
-                first_col = block_col + col
-                first_chunk_products(0, list(range(first_col, first_col + UNIT_COLS, N_TILE)))
-                if first_col + UNIT_COLS == COLS:
-                    first_chunk_products(1, list(range(0, COLS, N_TILE)))
-            elif g == PASSES - 1 and col + UNIT_COLS == BLOCK_COLS:
-                multiply_and_store(block, c, block_col)
+                multiply_unit(block, col, c, block_col, [0])
+                if block_col + col + UNIT_COLS == COLS:
+                    multiply_chunk(c, 1)
+            elif g == PASSES - 1:
+                multiply_unit(block, col, c, block_col, list(range(EXPERTS)))
 
         waiting = None
         for i, (c, g, col, block_col) in enumerate(units):
             if blocks[c, block_col] is None:
                 blocks[c, block_col] = new_block()
-            if waiting is not None and waiting[1] != c:
+            if waiting is not None and (waiting[1] != c or i == len(units) - 1):
                 finish(*waiting)
                 waiting = None
             grouped = regroup(raw[c, g], block_col + col, on_scalar=(i in SCALAR_UNITS))

@@ -46,7 +46,6 @@ def tile_flaxparallelexperts_t_e_kernel(
         grouped_pool = pools.enter_context(tc.tile_pool(name="grouped", bufs=4))
         quantised_pool = pools.enter_context(tc.tile_pool(name="quantised", bufs=3))
         psum = pools.enter_context(tc.psum_pool(name="psum", bufs=8))
-        pools.enter_context(tc.manual_schedule())
 
         w_codes = resident.tile([P, EXPERTS * PASSES, ROWS], U32, align_bytes=64)
         w_scales = resident.tile([P, ROWS], U8, align_bytes=64)

@@ -56,7 +56,7 @@ def tile_flaxparallelexperts_t_e_kernel(
             else:
                 raw = resident.tile([P, PACK, COLS], BF16, name="raw_c1_g%d" % g)
             rows = inputs[c, g * K_PASS : (g + 1) * K_PASS, :]
-            nc.sync.dma_start(out=raw[:], in_=rows.rearrange("(p j) w -> p j w", j=PACK))
+            nc.scalar.dma_start(out=raw[:], in_=rows.rearrange("(p j) w -> p j w", j=PACK))
             return raw
 
         def load_weights():

@@ -41,6 +41,7 @@ def tile_flaxparallelexperts_t_e_kernel(
 ):
     nc = tc.nc
     with ExitStack() as pools:
+        pools.enter_context(tc.manual_schedule())
         resident = pools.enter_context(tc.tile_pool(name="resident", bufs=1))
         arena = pools.enter_context(tc.tile_pool(name="arena", bufs=1))
         grouped_pool = pools.enter_context(tc.tile_pool(name="grouped", bufs=4))
@@ -181,12 +182,10 @@ def tile_flaxparallelexperts_t_e_kernel(
 
         nc.vector.memset(w_scales[:].bitcast(I32), 0)
 
+        load_weights()
         raw = {}
         raw[0, 0] = load_inputs(0, 0)
         raw[0, 1] = load_inputs(0, 1)
-        load_weights()
-        raw[1, 0] = load_inputs(1, 0)
-        raw[1, 1] = load_inputs(1, 1)
 
         halves = range(0, COLS, BLOCK_COLS)
         in_block = range(0, BLOCK_COLS, UNIT_COLS)
@@ -218,6 +217,9 @@ def tile_flaxparallelexperts_t_e_kernel(
                 finish(*waiting)
                 waiting = None
             grouped = regroup(raw[c, g], block_col + col, on_scalar=(i in SCALAR_UNITS))
+            if i == SCALAR_UNITS[0]:
+                raw[1, 0] = load_inputs(1, 0)
+                raw[1, 1] = load_inputs(1, 1)
             if waiting is not None:
                 finish(*waiting)
             waiting = (grouped, c, g, col, block_col)

@@ -109,25 +109,22 @@ def tile_flaxparallelexperts_t_e_kernel(
         staged_bytes = [0]
 
         def new_stage(width):
-            stage = []
-            for m in range(M_TILES):
-                first_byte = staged_bytes[0]
-                staged_bytes[0] = first_byte + width * 4
-                stage.append(
-                    arena.tile(
-                        [P, width],
-                        F32,
-                        name="stage_%d" % first_byte,
-                        offset=first_byte % ARENA_BYTES,
-                    )
-                )
-            return stage
-
-        def store(stage, c, e, m, first_col, width):
-            nc.sync.dma_start(
-                out=out[c * EXPERTS + e, m * P : (m + 1) * P, first_col : first_col + width],
-                in_=stage[m][:],
+            first_byte = staged_bytes[0]
+            staged_bytes[0] = first_byte + M_TILES * width * 4
+            return arena.tile(
+                [P, M_TILES, width],
+                F32,
+                name="stage_%d" % first_byte,
+                offset=first_byte % ARENA_BYTES,
             )
+
+        def store(stage, c, e, first_col, width):
+            rows = out[c * EXPERTS + e, :, first_col : first_col + width]
+            nc.sync.dma_start(out=rows.rearrange("(m p) w -> p m w", p=P), in_=stage[:])
+
+        def store_row_tile(stage, c, e, m, first_col, width):
+            rows = out[c * EXPERTS + e, m * P : (m + 1) * P, first_col : first_col + width]
+            nc.sync.dma_start(out=rows, in_=stage[:, m, :])
 
         def multiply_chunk(c, e):
             stage = new_stage(COLS)
@@ -137,8 +134,8 @@ def tile_flaxparallelexperts_t_e_kernel(
                     acc = psum.tile([P, N_TILE], F32, name="acc")
                     for g in range(PASSES):
                         one_pass(acc, block, e, m, g, n % BLOCK_COLS)
-                    nc.scalar.copy(out=stage[m][:, n : n + N_TILE], in_=acc[:])
-                store(stage, c, e, m, 0, COLS)
+                    nc.scalar.copy(out=stage[:, m, n : n + N_TILE], in_=acc[:])
+                store_row_tile(stage, c, e, m, 0, COLS)
 
         block_stages = {}
 
@@ -152,9 +149,11 @@ def tile_flaxparallelexperts_t_e_kernel(
                         acc = psum.tile([P, N_TILE], F32, name="acc")
                         for g in range(PASSES):
                             one_pass(acc, block, e, m, g, n)
-                        nc.scalar.copy(out=stage[m][:, n : n + N_TILE], in_=acc[:])
-                    if col + UNIT_COLS == BLOCK_COLS:
-                        store(stage, c, e, m, block_col, BLOCK_COLS)
+                        nc.scalar.copy(out=stage[:, m, n : n + N_TILE], in_=acc[:])
+                    if col + UNIT_COLS == BLOCK_COLS and c > 0 and e == 0:
+                        store_row_tile(stage, c, e, m, block_col, BLOCK_COLS)
+                if col + UNIT_COLS == BLOCK_COLS and not (c > 0 and e == 0):
+                    store(stage, c, e, block_col, BLOCK_COLS)
 
         open_groups = {}
 
@@ -172,13 +171,15 @@ def tile_flaxparallelexperts_t_e_kernel(
                         acc = open_groups[e, m, n]
                         one_pass(acc, block, e, m, g, n)
                         if g == PASSES - 1:
-                            dst = stage[m][:, n - col : n - col + N_TILE]
+                            dst = stage[:, m, n - col : n - col + N_TILE]
                             if last and n // N_TILE % 2 == 1:
                                 nc.vector.tensor_copy(out=dst, in_=acc[:])
                             else:
                                 nc.scalar.copy(out=dst, in_=acc[:])
-                    if g == PASSES - 1:
-                        store(stage, c, e, m, block_col + col, UNIT_COLS)
+                    if g == PASSES - 1 and e == 0:
+                        store_row_tile(stage, c, e, m, block_col + col, UNIT_COLS)
+                if g == PASSES - 1 and e > 0:
+                    store(stage, c, e, block_col + col, UNIT_COLS)
 
         nc.vector.memset(w_scales[:].bitcast(I32), 0)
 

@@ -118,9 +118,9 @@ def tile_flaxparallelexperts_t_e_kernel(
                 offset=first_byte % ARENA_BYTES,
             )
 
-        def store(stage, c, e, first_col, width):
+        def store(stage, c, e, first_col, width, queue):
             rows = out[c * EXPERTS + e, :, first_col : first_col + width]
-            nc.sync.dma_start(out=rows.rearrange("(m p) w -> p m w", p=P), in_=stage[:])
+            queue.dma_start(out=rows.rearrange("(m p) w -> p m w", p=P), in_=stage[:])
 
         def store_row_tile(stage, c, e, m, first_col, width):
             rows = out[c * EXPERTS + e, m * P : (m + 1) * P, first_col : first_col + width]
@@ -153,7 +153,7 @@ def tile_flaxparallelexperts_t_e_kernel(
                     if col + UNIT_COLS == BLOCK_COLS and c > 0 and e == 0:
                         store_row_tile(stage, c, e, m, block_col, BLOCK_COLS)
                 if col + UNIT_COLS == BLOCK_COLS and not (c > 0 and e == 0):
-                    store(stage, c, e, block_col, BLOCK_COLS)
+                    store(stage, c, e, block_col, BLOCK_COLS, nc.sync)
 
         open_groups = {}
 
@@ -179,7 +179,7 @@ def tile_flaxparallelexperts_t_e_kernel(
                     if g == PASSES - 1 and e == 0:
                         store_row_tile(stage, c, e, m, block_col + col, UNIT_COLS)
                 if g == PASSES - 1 and e > 0:
-                    store(stage, c, e, block_col + col, UNIT_COLS)
+                    store(stage, c, e, block_col + col, UNIT_COLS, nc.scalar)
 
         nc.vector.memset(w_scales[:].bitcast(I32), 0)
 

from contextlib import ExitStack

import concourse.mybir as mybir

BF16 = mybir.dt.bfloat16
F32 = mybir.dt.float32
I32 = mybir.dt.int32
U32 = mybir.dt.uint32
U8 = mybir.dt.uint8
FP8X4 = mybir.dt.float8_e4m3fn_x4

P = 128
PACK = 4
K_PASS = P * PACK

CHUNKS = 2
EXPERTS = 2
K = 1024
ROWS = 256
COLS = 4096
PASSES = K // K_PASS
M_TILES = ROWS // P

N_TILE = 512
UNIT_COLS = 1024
BLOCK_COLS = 2048
UNITS = COLS // UNIT_COLS

RAW_BYTES = PACK * COLS * 2
ARENA_BYTES = PASSES * RAW_BYTES

SCALAR_UNITS = (1, 3, 5)

RUN = 4

FLOPS = 2 * CHUNKS * EXPERTS * ROWS * K * COLS


def tile_flaxparallelexperts_t_e_kernel(
    tc, inputs, weight_words, weight_scales, expert_size, out
):
    nc = tc.nc
    with ExitStack() as pools:
        pools.enter_context(tc.manual_schedule())
        resident = pools.enter_context(tc.tile_pool(name="resident", bufs=1))
        arena = pools.enter_context(tc.tile_pool(name="arena", bufs=1))
        grouped_pool = pools.enter_context(tc.tile_pool(name="grouped", bufs=4))
        quantised_pool = pools.enter_context(tc.tile_pool(name="quantised", bufs=3))
        psum = pools.enter_context(tc.psum_pool(name="psum", bufs=8))

        w_codes = resident.tile([P, EXPERTS * PASSES, ROWS], U32, align_bytes=64)
        w_scales = resident.tile([P, ROWS], U8, align_bytes=64)

        def load_inputs(c, g):
            if c == 0:
                raw = arena.tile([P, PACK, COLS], BF16, name="raw_c0_g%d" % g, offset=g * RAW_BYTES)
            else:
                raw = resident.tile([P, PACK, COLS], BF16, name="raw_c1_g%d" % g)
            rows = inputs[c, g * K_PASS : (g + 1) * K_PASS, :]
            nc.scalar.dma_start(out=raw[:], in_=rows.rearrange("(p j) w -> p j w", j=PACK))
            return raw

        def load_weights():
            nc.sync.dma_start(
                out=w_codes[:].bitcast(I32),
                in_=weight_words.rearrange("g p n t -> p g (n t)").bitcast(I32),
            )
            for quadrant in range(4):
                nc.sync.dma_start(
                    out=w_scales[32 * quadrant : 32 * quadrant + 16].bitcast(I32),
                    in_=weight_scales[:, 4 * quadrant : 4 * quadrant + 4, :].bitcast(I32),
                )

        def regroup(raw, col, on_scalar):
            grouped = grouped_pool.tile([P, UNIT_COLS, PACK], BF16, align_bytes=64, name="grouped")
            dst = grouped[:].rearrange("p (w i) j -> p w j i", i=RUN)
            src = raw[:, :, col : col + UNIT_COLS].rearrange("p j (w i) -> p w j i", i=RUN)
            if on_scalar:
                nc.scalar.copy(out=dst, in_=src)
            else:
                nc.vector.tensor_copy(out=dst, in_=src)
            return grouped

        def new_block():
            x_codes = quantised_pool.tile([P, PASSES, BLOCK_COLS], U32, align_bytes=64, name="x_codes")
            x_scales = quantised_pool.tile([P, PASSES, BLOCK_COLS], U8, align_bytes=64, name="x_scales")
            return x_codes, x_scales

        def quantise(grouped, block, g, col):
            x_codes, x_scales = block
            nc.vector.quantize_mx(
                out=x_codes[:, g, col : col + UNIT_COLS].bitcast(FP8X4),
                scales=x_scales[:, g, col : col + UNIT_COLS],
                in_=grouped[:].rearrange("p w j -> p (w j)"),
            )

        def one_pass(acc, block, e, m, g, n):
            x_codes, x_scales = block
            nc.tensor.matmul_mx(
                out=acc[:],
                lhsT=w_codes[:, e * PASSES + g, m * P : (m + 1) * P].bitcast(FP8X4),
                lhsT_scale=w_scales[4 * (e * PASSES + g) :, m * P : (m + 1) * P],
                rhs=x_codes[:, g, n : n + N_TILE].bitcast(FP8X4),
                rhs_scale=x_scales[:, g, n : n + N_TILE],
                start=(g == 0),
                stop=(g == PASSES - 1),
            )

        staged_bytes = [0]

        def new_stage(width):
            first_byte = staged_bytes[0]
            staged_bytes[0] = first_byte + M_TILES * width * 4
            return arena.tile(
                [P, M_TILES, width],
                F32,
                name="stage_%d" % first_byte,
                offset=first_byte % ARENA_BYTES,
            )

        def store(stage, c, e, first_col, width, queue):
            rows = out[c * EXPERTS + e, :, first_col : first_col + width]
            queue.dma_start(out=rows.rearrange("(m p) w -> p m w", p=P), in_=stage[:])

        def store_row_tile(stage, c, e, m, first_col, width):
            rows = out[c * EXPERTS + e, m * P : (m + 1) * P, first_col : first_col + width]
            nc.sync.dma_start(out=rows, in_=stage[:, m, :])

        def multiply_chunk(c, e):
            stage = new_stage(COLS)
            for m in range(M_TILES):
                for n in range(0, COLS, N_TILE):
                    block = blocks[c, n // BLOCK_COLS * BLOCK_COLS]
                    acc = psum.tile([P, N_TILE], F32, name="acc")
                    for g in range(PASSES):
                        one_pass(acc, block, e, m, g, n % BLOCK_COLS)
                    nc.scalar.copy(out=stage[:, m, n : n + N_TILE], in_=acc[:])
                store_row_tile(stage, c, e, m, 0, COLS)

        block_stages = {}

        def multiply_unit(block, col, c, block_col, experts):
            for e in experts:
                if col == 0:
                    block_stages[e] = new_stage(BLOCK_COLS)
                stage = block_stages[e]
                for m in range(M_TILES):
                    for n in range(col, col + UNIT_COLS, N_TILE):
                        acc = psum.tile([P, N_TILE], F32, name="acc")
                        for g in range(PASSES):
                            one_pass(acc, block, e, m, g, n)
                        nc.scalar.copy(out=stage[:, m, n : n + N_TILE], in_=acc[:])
                    if col + UNIT_COLS == BLOCK_COLS and c > 0 and e == 0:
                        store_row_tile(stage, c, e, m, block_col, BLOCK_COLS)
                if col + UNIT_COLS == BLOCK_COLS and not (c > 0 and e == 0):
                    store(stage, c, e, block_col, BLOCK_COLS, nc.sync)

        open_groups = {}

        def follow(block, g, col, c, block_col):
            last = col + UNIT_COLS == BLOCK_COLS
            for e in range(EXPERTS):
                stage = None
                if g == PASSES - 1:
                    stage = new_stage(UNIT_COLS)
                for m in range(M_TILES):
                    for n in range(col, col + UNIT_COLS, N_TILE):
                        if g == 0:
                            acc = psum.tile([P, N_TILE], F32, name="acc")
                            open_groups[e, m, n] = acc
                        acc = open_groups[e, m, n]
                        one_pass(acc, block, e, m, g, n)
                        if g == PASSES - 1:
                            dst = stage[:, m, n - col : n - col + N_TILE]
                            if last and n // N_TILE % 2 == 1:
                                nc.vector.tensor_copy(out=dst, in_=acc[:])
                            else:
                                nc.scalar.copy(out=dst, in_=acc[:])
                    if g == PASSES - 1 and e == 0:
                        store_row_tile(stage, c, e, m, block_col + col, UNIT_COLS)
                if g == PASSES - 1 and e > 0:
                    store(stage, c, e, block_col + col, UNIT_COLS, nc.scalar)

        nc.vector.memset(w_scales[:].bitcast(I32), 0)

        load_weights()
        raw = {}
        raw[0, 0] = load_inputs(0, 0)
        raw[0, 1] = load_inputs(0, 1)

        halves = range(0, COLS, BLOCK_COLS)
        in_block = range(0, BLOCK_COLS, UNIT_COLS)
        blocks = {}
        for c in range(CHUNKS):
            for block_col in halves:
                blocks[c, block_col] = None
        units = [(0, g, col, block_col) for g in range(PASSES) for block_col in halves for col in in_block]
        units += [(1, g, col, 0) for g in range(PASSES) for col in in_block]
        units += [(1, g, col, BLOCK_COLS) for col in in_block for g in range(PASSES)]

        def finish(grouped, c, g, col, block_col):
            block = blocks[c, block_col]
            quantise(grouped, block, g, col)
            if (c, block_col) == (CHUNKS - 1, COLS - BLOCK_COLS):
                follow(block, g, col, c, block_col)
            elif c == 0 and g == PASSES - 1:
                multiply_unit(block, col, c, block_col, [0])
                if block_col + col + UNIT_COLS == COLS:
                    multiply_chunk(c, 1)
            elif g == PASSES - 1:
                multiply_unit(block, col, c, block_col, list(range(EXPERTS)))

        waiting = None
        for i, (c, g, col, block_col) in enumerate(units):
            if blocks[c, block_col] is None:
                blocks[c, block_col] = new_block()
            if waiting is not None and (waiting[1] != c or i == len(units) - 1):
                finish(*waiting)
                waiting = None
            grouped = regroup(raw[c, g], block_col + col, on_scalar=(i in SCALAR_UNITS))
            if i == SCALAR_UNITS[0]:
                raw[1, 0] = load_inputs(1, 0)
                raw[1, 1] = load_inputs(1, 1)
            if waiting is not None:
                finish(*waiting)
            waiting = (grouped, c, g, col, block_col)
        finish(*waiting)
